import numpy as np
import ml_dtypes


def mxq(x, axis, fmt="e4m3"):
    dtype, down = {"e4m3": (ml_dtypes.float8_e4m3fn, 7), "e5m2": (ml_dtypes.float8_e5m2, 14)}[fmt]
    v = np.moveaxis(np.asarray(x, np.float32).astype(ml_dtypes.bfloat16).astype(np.float64), axis, -1)
    blocks = v.reshape(v.shape[:-1] + (-1, 32))
    amax = np.abs(blocks).max(-1, keepdims=True)
    byte = np.maximum(np.where(amax > 0, np.frexp(amax)[1] - 1 + 127, 0) - down, 1)
    scale = np.exp2(byte - 127.0)
    codes = (blocks / scale).astype(np.float32).astype(dtype).astype(np.float64)
    return np.moveaxis((codes * scale).reshape(v.shape), -1, axis)


WIDE = False


def mx_kscale(k):
    if not WIDE:
        return np.ones(k)
    levels = np.array([10, -10, 5, -5, 0])
    if k % 512:
        return np.exp2(np.random.permutation(np.resize(levels, k // 32))).repeat(32)
    a = np.empty((k // 512, 16))
    for p in range(k // 512):
        a[p, :8] = np.random.permutation(np.resize(levels, 8))
        for g in range(8):
            far = levels[np.abs(levels - a[p, g]) >= 10]
            a[p, g + 8] = far[np.random.randint(len(far))]
    return np.exp2(a.ravel()).repeat(32)


BF16 = ml_dtypes.bfloat16


def bf(x):
    return np.asarray(x, np.float32).astype(BF16)


def f64(x):
    return np.asarray(x).astype(np.float64)


B, S, H, NH, FF = 8, 512, 1024, 8, 1024
EPS = 1e-7


def layer_norm(x, g, b):
    m = x.mean(-1, keepdims=True)
    v = ((x - m) ** 2).mean(-1, keepdims=True)
    return (x - m) / np.sqrt(v + EPS) * g + b


def setup_inputs():
    s = mx_kscale(FF)
    r = np.random.standard_normal
    return {"ff": bf(r((B, S, FF)) * 0.65 * s), "attn_out": bf(r((B, S, H))),
            "Wf": bf(r((FF, H)) * 1.5 / np.sqrt(FF) / s[:, None]), "b_f": bf(r(H) * 0.2),
            "ln2_g": bf(1.0 + 0.1 * r(H)), "ln2_b": bf(0.1 * r(H))}


def reference(ff, attn_out, Wf, b_f, ln2_g, ln2_b):
    u = (mxq(f64(ff), 2, "e4m3") @ mxq(f64(Wf), 0, "e4m3")) + f64(b_f) + f64(attn_out)
    return layer_norm(u, f64(ln2_g), f64(ln2_b))

@@ -1,0 +1,272 @@
+from contextlib import ExitStack
+
+import concourse.mybir as mybir
+from concourse.masks import make_identity
+
+F32 = mybir.dt.float32
+BF16 = mybir.dt.bfloat16
+I32 = mybir.dt.int32
+U32 = mybir.dt.uint32
+U8 = mybir.dt.uint8
+FP8X4 = mybir.dt.float8_e4m3fn_x4
+ALU = mybir.AluOpType
+ACT = mybir.ActivationFunctionType
+
+P = 128
+PACK = 4
+K_PASS = P * PACK
+TOKENS, K, H = 8 * 512, 1024, 1024
+PASSES = K // K_PASS
+N_TILES = TOKENS // P
+GROUP = 4
+BANK = 512
+HALVES = H // BANK
+EPS = 1e-7
+
+FLOPS = 2 * TOKENS * K * H
+PREP = GROUP + 2
+FF_AHEAD = PREP + 4
+RES_AHEAD = 4
+HAND_OVER = 4
+
+
+def tile_disentangledattention_pc_t_kernel(tc, ff, attn_out, Wf, b_f, ln2_g, ln2_b, out):
+    nc = tc.nc
+    ff_v = ff.rearrange("b s f -> (b s) f").rearrange("(i p) f -> i p f", p=P)
+    res_v = attn_out.rearrange("b s f -> (b s) f").rearrange("(i p) f -> i p f", p=P)
+    out_v = out.rearrange("b s f -> (b s) f").rearrange("(i p) f -> i p f", p=P)
+    w_v = Wf.rearrange("(g p t) n -> g p t n", p=P, t=PACK)
+
+    with ExitStack() as ctx:
+        const = ctx.enter_context(tc.tile_pool(name="const", bufs=1))
+        weights = ctx.enter_context(tc.tile_pool(name="weights", bufs=1))
+        ff_pool = ctx.enter_context(tc.tile_pool(name="ff_pool", bufs=FF_AHEAD))
+        res_pool = ctx.enter_context(tc.tile_pool(name="res_pool", bufs=RES_AHEAD + 1))
+        quant = ctx.enter_context(tc.tile_pool(name="quant", bufs=2))
+        work = ctx.enter_context(tc.tile_pool(name="work", bufs=4))
+        y_pool = ctx.enter_context(tc.tile_pool(name="y_pool", bufs=6))
+        stats = ctx.enter_context(tc.tile_pool(name="stats", bufs=4))
+        psum_const = ctx.enter_context(tc.psum_pool(name="psum_const", bufs=1))
+        psum_t = ctx.enter_context(tc.psum_pool(name="psum_t", bufs=2))
+        psum_acc = ctx.enter_context(tc.psum_pool(name="psum_acc", bufs=4))
+        ctx.enter_context(tc.manual_schedule())
+
+        def half(h):
+            return slice(h * BANK, (h + 1) * BANK)
+
+        ff_sb, res_sb, xt, grouped, codes = {}, {}, {}, {}, {}
+        rb, acc, u, negmean, ssq, rstd, y = {}, {}, {}, {}, {}, {}, {}
+
+        def load_ff(i):
+            ff_sb[i] = ff_pool.tile([P, K], BF16, name="ff_sb")
+            nc.sync.dma_start(out=ff_sb[i][:], in_=ff_v[i])
+
+        def load_res(i):
+            res_sb[i] = res_pool.tile([P, H], BF16, name="res_sb")
+            nc.sync.dma_start(out=res_sb[i][:], in_=res_v[i])
+
+        def transpose(i):
+            words = ff_sb[i][:].bitcast(F32)
+            xt[i] = psum_t.tile([P, PASSES * 2, P], F32, name="xt")
+            for g in range(PASSES):
+                for u2 in range(2):
+                    nc.tensor.transpose(xt[i][:, 2 * g + u2, :], words[:, 2 * P * g + u2 : 2 * P * (g + 1) : 2], ident[:])
+
+        def regroup(i):
+            if i % GROUP == 0:
+                grouped[i // GROUP] = quant.tile([P, GROUP, PASSES, P, PACK], BF16, align_bytes=64, name="grouped")
+            nc.scalar.copy(
+                out=grouped[i // GROUP][:, i % GROUP].bitcast(F32),
+                in_=xt[i][:].rearrange("p (g u) r -> p g r u", u=2),
+            )
+
+        def quantise_ff(n):
+            ff_codes = quant.tile([P, GROUP * PASSES * P], U32, align_bytes=64)
+            ff_scales = quant.tile([P, GROUP * PASSES * P], U8, align_bytes=64)
+            nc.vector.quantize_mx(
+                out=ff_codes[:].bitcast(FP8X4),
+                scales=ff_scales[:],
+                in_=grouped[n][:].rearrange("p j g r t -> p (j g r t)"),
+            )
+            codes[n] = (ff_codes, ff_scales)
+
+        def add_bias(i):
+            rb[i] = work.tile([P, H], F32, name="rb")
+            nc.gpsimd.tensor_tensor(out=rb[i][:], in0=res_sb[i][:], in1=bias_bc[:], op=ALU.add)
+
+        def project(i):
+            ff_codes, ff_scales = codes[i // GROUP]
+            for h in range(HALVES):
+                acc[i, h] = psum_acc.tile([P, BANK], F32, name="acc")
+                for g in range(PASSES):
+                    tok = slice(((i % GROUP) * PASSES + g) * P, ((i % GROUP) * PASSES + g + 1) * P)
+                    nc.tensor.matmul_mx(
+                        out=acc[i, h][:],
+                        lhsT=ff_codes[:, tok].bitcast(FP8X4),
+                        lhsT_scale=ff_scales[:, tok],
+                        rhs=w_codes[:, g, half(h)].bitcast(FP8X4),
+                        rhs_scale=w_scales[:, g, half(h)],
+                        start=(g == 0),
+                        stop=(g == PASSES - 1),
+                    )
+
+        def add_residual(i, h):
+            if h == 0:
+                u[i] = work.tile([P, H], F32, name="u")
+            nc.vector.tensor_tensor(out=u[i][:, half(h)], in0=acc[i, h][:], in1=rb[i][:, half(h)], op=ALU.add)
+
+        def mean(i):
+            negmean[i] = stats.tile([P, 1], F32, name="negmean")
+            unused = stats.tile([P, H], BF16, name="unused")
+            nc.scalar.activation(out=unused[:], in_=u[i][:], func=ACT.Identity, scale=-1.0 / H, accum_out=negmean[i][:])
+
+        def squared_deviations(i):
+            ssq[i] = stats.tile([P, 1], F32, name="ssq")
+            unused = stats.tile([P, H], BF16, name="unused")
+            nc.scalar.activation(out=unused[:], in_=u[i][:], func=ACT.Square, bias=negmean[i][:], scale=1.0, accum_out=ssq[i][:])
+
+        def inverse_deviation(i):
+            rstd[i] = stats.tile([P, 1], F32, name="rstd")
+            nc.scalar.activation(out=rstd[i][:], in_=ssq[i][:], func=ACT.Abs_reciprocal_sqrt, bias=eps_t[:], scale=1.0 / H)
+
+        def centre_and_gain(i):
+            y[i] = y_pool.tile([P, H], F32, name="y")
+            nc.vector.scalar_tensor_tensor(out=y[i][:], in0=u[i][:], scalar=negmean[i][:], in1=gain_ps[:], op0=ALU.add, op1=ALU.mult)
+
+        def scale_and_shift(i):
+            nc.vector.scalar_tensor_tensor(out=y[i][:], in0=y[i][:], scalar=rstd[i][:], in1=shift_ps[:], op0=ALU.mult, op1=ALU.add)
+
+        def scale_only(i):
+            nc.scalar.activation(out=y[i][:], in_=y[i][:], func=ACT.Copy, scale=rstd[i][:])
+
+        def shift_only(i):
+            nc.gpsimd.tensor_tensor(out=y[i][:], in0=y[i][:], in1=shift_bc[:], op=ALU.add)
+
+        def store(i):
+            nc.sync.dma_start(out=out_v[i], in_=y[i][:])
+
+        ident = const.tile([P, P], F32)
+        make_identity(nc, ident[:])
+        ones = const.tile([P, P], BF16)
+        nc.vector.memset(ones[:], 1.0)
+        rows = {}
+        for name in ("bias", "gain", "shift"):
+            rows[name] = const.tile([P, H], BF16, name="row_" + name)
+            nc.vector.memset(rows[name][:].bitcast(I32), 0)
+        eps_t = const.tile([P, 1], F32)
+        nc.vector.memset(eps_t[:], EPS)
+        warm = const.tile([P, 1], F32)
+        nc.scalar.activation(out=warm[:], in_=eps_t[:], func=ACT.Abs_reciprocal_sqrt)
+
+        def load_row(name, vec):
+            nc.sync.dma_start(out=rows[name][0:1, :], in_=vec.rearrange("(o n) -> o n", o=1))
+
+        def spread_row(name, h, out_ps):
+            nc.tensor.matmul(out=out_ps, lhsT=ones[:], rhs=rows[name][:, half(h)], start=True, stop=True)
+
+        w_raw = weights.tile([P, PASSES, PACK, H], BF16)
+
+        def load_w(g, h):
+            nc.sync.dma_start(out=w_raw[:, g, :, half(h)], in_=w_v[g][:, :, half(h)])
+
+        load_w(0, 0)
+        load_row("bias", b_f)
+        load_w(1, 0)
+        load_res(0)
+        load_w(0, 1)
+        load_w(1, 1)
+        for i in range(GROUP):
+            load_ff(i)
+        for i in range(1, RES_AHEAD):
+            load_res(i)
+        load_row("gain", ln2_g)
+        load_row("shift", ln2_b)
+        for i in range(GROUP, FF_AHEAD):
+            load_ff(i)
+
+        bias_bc = const.tile([P, H], BF16)
+        for h in range(HALVES):
+            bias_ps = psum_acc.tile([P, BANK], F32, name="acc")
+            spread_row("bias", h, bias_ps[:])
+            nc.scalar.copy(out=bias_bc[:, half(h)], in_=bias_ps[:])
+        add_bias(0)
+
+        w_grp = weights.tile([P, PASSES, H, PACK], BF16, align_bytes=64)
+        w_codes = weights.tile([P, PASSES, H], U32, align_bytes=64)
+        w_scales = weights.tile([P, PASSES, H], U8, align_bytes=64)
+
+        def regroup_w(g, h):
+            nc.vector.tensor_copy(
+                out=w_grp[:, g, half(h), :].rearrange("p (c i) t -> p c t i", i=4),
+                in_=w_raw[:, g, :, half(h)].rearrange("p t (c i) -> p c t i", i=4),
+            )
+
+        def quantise_w(g, h):
+            nc.vector.quantize_mx(
+                out=w_codes[:, g, half(h)].bitcast(FP8X4),
+                scales=w_scales[:, g, half(h)],
+                in_=w_grp[:, g, half(h), :].rearrange("p n t -> p (n t)"),
+            )
+
+        for h in range(HALVES):
+            for g in range(PASSES):
+                regroup_w(g, h)
+            for g in range(PASSES):
+                quantise_w(g, h)
+
+        for i in range(GROUP):
+            transpose(i)
+            regroup(i)
+        quantise_ff(0)
+
+        gain_ps = psum_const.tile([P, H], BF16)
+        shift_ps = psum_const.tile([P, H], BF16)
+        for h in range(HALVES):
+            spread_row("gain", h, gain_ps[:, half(h)])
+            spread_row("shift", h, shift_ps[:, half(h)])
+        shift_bc = const.tile([P, H], BF16)
+        nc.scalar.copy(out=shift_bc[:], in_=shift_ps[:])
+
+        for i in range(GROUP, PREP):
+            transpose(i)
+            regroup(i)
+
+        def tile_exists(i):
+            return 0 <= i < N_TILES
+
+        def handed_over(i):
+            return tile_exists(i) and i % HAND_OVER == 1
+
+        for i in range(N_TILES + 4):
+            if tile_exists(i + FF_AHEAD):
+                load_ff(i + FF_AHEAD)
+            if tile_exists(i + RES_AHEAD):
+                load_res(i + RES_AHEAD)
+            if tile_exists(i + 1):
+                add_bias(i + 1)
+            if tile_exists(i):
+                project(i)
+            if tile_exists(i + PREP):
+                transpose(i + PREP)
+                regroup(i + PREP)
+            if handed_over(i - 3):
+                scale_only(i - 3)
+            if tile_exists(i):
+                add_residual(i, 0)
+            if tile_exists(i - 2):
+                centre_and_gain(i - 2)
+            if tile_exists(i):
+                add_residual(i, 1)
+                mean(i)
+            if tile_exists(i - 1):
+                inverse_deviation(i - 1)
+            if tile_exists(i):
+                squared_deviations(i)
+            if tile_exists(i - 3) and not handed_over(i - 3):
+                scale_and_shift(i - 3)
+                store(i - 3)
+            if handed_over(i - 4):
+                shift_only(i - 4)
+                store(i - 4)
+            if i % GROUP == GROUP - 2 and tile_exists(i + 2):
+                quantise_ff((i + 2) // GROUP)

@@ -22,12 +22,27 @@ GROUP = 4
 BANK = 512
 HALVES = H // BANK
 EPS = 1e-7
-
 FLOPS = 2 * TOKENS * K * H
-PREP = GROUP + 2
-FF_AHEAD = PREP + 4
-RES_AHEAD = 4
-HAND_OVER = 4
+QLEAD = 1
+PREP = GROUP + 1
+FF_AHEAD = PREP + 3
+RB_AHEAD = 2
+RES_AHEAD = RB_AHEAD + 3
+G1_LAG = 1
+G2_LAG = 2
+SHIFT_LAG = 3
+GSPLIT = 1
+SREG = ((0, 1),)
+HEAD_T = 2
+def handed_over(i): return 0 <= i < N_TILES - 1 and i % 8 in (1,3,4,6,7)
+def by_tensor(i): return i % 3 == 0 and i < 33
+def sum_on_vector(i): return True
+def qplace(i): return 'mid'
+ORDER = 'd0 d1 g1 q g2'
+ORDER = 'q d0 d1 g1 g2'
+RB_AHEAD = 3
+RES_AHEAD = RB_AHEAD + 3
+GSPLIT = 2
 
 
 def tile_disentangledattention_pc_t_kernel(tc, ff, attn_out, Wf, b_f, ln2_g, ln2_b, out):
@@ -36,13 +51,13 @@ def tile_disentangledattention_pc_t_kernel(tc, ff, attn_out, Wf, b_f, ln2_g, ln2
     res_v = attn_out.rearrange("b s f -> (b s) f").rearrange("(i p) f -> i p f", p=P)
     out_v = out.rearrange("b s f -> (b s) f").rearrange("(i p) f -> i p f", p=P)
     w_v = Wf.rearrange("(g p t) n -> g p t n", p=P, t=PACK)
-
     with ExitStack() as ctx:
         const = ctx.enter_context(tc.tile_pool(name="const", bufs=1))
         weights = ctx.enter_context(tc.tile_pool(name="weights", bufs=1))
         ff_pool = ctx.enter_context(tc.tile_pool(name="ff_pool", bufs=FF_AHEAD))
         res_pool = ctx.enter_context(tc.tile_pool(name="res_pool", bufs=RES_AHEAD + 1))
         quant = ctx.enter_context(tc.tile_pool(name="quant", bufs=2))
+        rb_pool = ctx.enter_context(tc.tile_pool(name="rb_pool", bufs=RB_AHEAD + 1))
         work = ctx.enter_context(tc.tile_pool(name="work", bufs=4))
         y_pool = ctx.enter_context(tc.tile_pool(name="y_pool", bufs=6))
         stats = ctx.enter_context(tc.tile_pool(name="stats", bufs=4))
@@ -55,7 +70,7 @@ def tile_disentangledattention_pc_t_kernel(tc, ff, attn_out, Wf, b_f, ln2_g, ln2
             return slice(h * BANK, (h + 1) * BANK)
 
         ff_sb, res_sb, xt, grouped, codes = {}, {}, {}, {}, {}
-        rb, acc, u, negmean, ssq, rstd, y = {}, {}, {}, {}, {}, {}, {}
+        rb, acc, u, total, negmean, ssq, rstd, y = {}, {}, {}, {}, {}, {}, {}, {}
 
         def load_ff(i):
             ff_sb[i] = ff_pool.tile([P, K], BF16, name="ff_sb")
@@ -80,19 +95,31 @@ def tile_disentangledattention_pc_t_kernel(tc, ff, attn_out, Wf, b_f, ln2_g, ln2
                 in_=xt[i][:].rearrange("p (g u) r -> p g r u", u=2),
             )
 
-        def quantise_ff(n):
-            ff_codes = quant.tile([P, GROUP * PASSES * P], U32, align_bytes=64)
-            ff_scales = quant.tile([P, GROUP * PASSES * P], U8, align_bytes=64)
+        def quantise_ff(n, first, last):
+            if first == 0:
+                ff_codes = quant.tile([P, GROUP * PASSES * P], U32, align_bytes=64)
+                ff_scales = quant.tile([P, GROUP * PASSES * P], U8, align_bytes=64)
+                codes[n] = (ff_codes, ff_scales)
+            c = slice(first * PASSES * P, last * PASSES * P)
             nc.vector.quantize_mx(
-                out=ff_codes[:].bitcast(FP8X4),
-                scales=ff_scales[:],
-                in_=grouped[n][:].rearrange("p j g r t -> p (j g r t)"),
+                out=codes[n][0][:, c].bitcast(FP8X4),
+                scales=codes[n][1][:, c],
+                in_=grouped[n][:, first:last].rearrange("p j g r t -> p (j g r t)"),
             )
-            codes[n] = (ff_codes, ff_scales)
 
         def add_bias(i):
-            rb[i] = work.tile([P, H], F32, name="rb")
-            nc.gpsimd.tensor_tensor(out=rb[i][:], in0=res_sb[i][:], in1=bias_bc[:], op=ALU.add)
+            rb[i] = rb_pool.tile([P, H], F32, name="rb")
+            if by_tensor(i):
+                for h in range(HALVES):
+                    ps = psum_acc.tile([P, BANK], F32, name="acc")
+                    nc.tensor.matmul(out=ps[:], lhsT=ident_bf[:], rhs=res_sb[i][:, half(h)], start=True, stop=False)
+                    nc.tensor.matmul(out=ps[:], lhsT=ones[:], rhs=rows["bias"][:, half(h)], start=False, stop=True)
+                    nc.scalar.copy(out=rb[i][:, half(h)], in_=ps[:])
+                return
+            w = H // GSPLIT
+            for s in range(GSPLIT):
+                c = slice(s * w, s * w + w)
+                nc.gpsimd.tensor_tensor(out=rb[i][:, c], in0=res_sb[i][:, c], in1=bias_bc[:, c], op=ALU.add)
 
         def project(i):
             ff_codes, ff_scales = codes[i // GROUP]
@@ -104,8 +131,8 @@ def tile_disentangledattention_pc_t_kernel(tc, ff, attn_out, Wf, b_f, ln2_g, ln2
                         out=acc[i, h][:],
                         lhsT=ff_codes[:, tok].bitcast(FP8X4),
                         lhsT_scale=ff_scales[:, tok],
-                        rhs=w_codes[:, g, half(h)].bitcast(FP8X4),
-                        rhs_scale=w_scales[:, g, half(h)],
+                        rhs=w_codes[g, h][:].bitcast(FP8X4),
+                        rhs_scale=w_scales[g, h][:],
                         start=(g == 0),
                         stop=(g == PASSES - 1),
                     )
@@ -113,12 +140,20 @@ def tile_disentangledattention_pc_t_kernel(tc, ff, attn_out, Wf, b_f, ln2_g, ln2
         def add_residual(i, h):
             if h == 0:
                 u[i] = work.tile([P, H], F32, name="u")
-            nc.vector.tensor_tensor(out=u[i][:, half(h)], in0=acc[i, h][:], in1=rb[i][:, half(h)], op=ALU.add)
+                total[i] = stats.tile([P, HALVES], F32, name="total")
+            if sum_on_vector(i):
+                nc.vector.scalar_tensor_tensor(out=u[i][:, half(h)], in0=acc[i, h][:], scalar=1.0, in1=rb[i][:, half(h)], op0=ALU.mult, op1=ALU.add, accum_out=total[i][:, h:h+1])
+            else:
+                nc.vector.tensor_tensor(out=u[i][:, half(h)], in0=acc[i, h][:], in1=rb[i][:, half(h)], op=ALU.add)
 
         def mean(i):
             negmean[i] = stats.tile([P, 1], F32, name="negmean")
-            unused = stats.tile([P, H], BF16, name="unused")
-            nc.scalar.activation(out=unused[:], in_=u[i][:], func=ACT.Identity, scale=-1.0 / H, accum_out=negmean[i][:])
+            if sum_on_vector(i):
+                unused = stats.tile([P, HALVES], F32, name="unused2")
+                nc.scalar.activation(out=unused[:], in_=total[i][:], func=ACT.Identity, scale=-1.0 / H, accum_out=negmean[i][:])
+            else:
+                unused = stats.tile([P, H], BF16, name="unused")
+                nc.scalar.activation(out=unused[:], in_=u[i][:], func=ACT.Identity, scale=-1.0 / H, accum_out=negmean[i][:])
 
         def squared_deviations(i):
             ssq[i] = stats.tile([P, 1], F32, name="ssq")
@@ -140,16 +175,21 @@ def tile_disentangledattention_pc_t_kernel(tc, ff, attn_out, Wf, b_f, ln2_g, ln2
             nc.scalar.activation(out=y[i][:], in_=y[i][:], func=ACT.Copy, scale=rstd[i][:])
 
         def shift_only(i):
-            nc.gpsimd.tensor_tensor(out=y[i][:], in0=y[i][:], in1=shift_bc[:], op=ALU.add)
+            w = H // GSPLIT
+            for s in range(GSPLIT):
+                c = slice(s * w, s * w + w)
+                nc.gpsimd.tensor_tensor(out=y[i][:, c], in0=y[i][:, c], in1=shift_bc[:, c], op=ALU.add)
 
         def store(i):
             nc.sync.dma_start(out=out_v[i], in_=y[i][:])
 
+        rows = {}
         ident = const.tile([P, P], F32)
         make_identity(nc, ident[:])
+        ident_bf = const.tile([P, P], BF16)
+        nc.scalar.copy(out=ident_bf[:], in_=ident[:])
         ones = const.tile([P, P], BF16)
         nc.vector.memset(ones[:], 1.0)
-        rows = {}
         for name in ("bias", "gain", "shift"):
             rows[name] = const.tile([P, H], BF16, name="row_" + name)
             nc.vector.memset(rows[name][:].bitcast(I32), 0)
@@ -164,109 +204,133 @@ def tile_disentangledattention_pc_t_kernel(tc, ff, attn_out, Wf, b_f, ln2_g, ln2
         def spread_row(name, h, out_ps):
             nc.tensor.matmul(out=out_ps, lhsT=ones[:], rhs=rows[name][:, half(h)], start=True, stop=True)
 
-        w_raw = weights.tile([P, PASSES, PACK, H], BF16)
+        w_raw, w_grp, w_codes, w_scales = {}, {}, {}, {}
+        for h in range(HALVES):
+            for g in range(PASSES):
+                w_raw[g, h] = weights.tile([P, PACK, BANK], BF16, name="w_raw%d%d" % (g, h))
+                w_grp[g, h] = weights.tile([P, BANK, PACK], BF16, align_bytes=64, name="w_grp%d%d" % (g, h))
+                w_codes[g, h] = weights.tile([P, BANK], U32, align_bytes=64, name="w_codes%d%d" % (g, h))
+                w_scales[g, h] = weights.tile([P, BANK], U8, align_bytes=64, name="w_scales%d%d" % (g, h))
 
         def load_w(g, h):
-            nc.sync.dma_start(out=w_raw[:, g, :, half(h)], in_=w_v[g][:, :, half(h)])
+            nc.sync.dma_start(out=w_raw[g, h][:], in_=w_v[g][:, :, half(h)])
 
         load_w(0, 0)
-        load_row("bias", b_f)
+        load_ff(0)
         load_w(1, 0)
-        load_res(0)
         load_w(0, 1)
         load_w(1, 1)
-        for i in range(GROUP):
-            load_ff(i)
-        for i in range(1, RES_AHEAD):
-            load_res(i)
+        load_res(0)
+        load_row("bias", b_f)
+        load_ff(1)
+        load_res(1)
+        load_ff(2)
+        load_ff(3)
+        load_res(2)
         load_row("gain", ln2_g)
         load_row("shift", ln2_b)
         for i in range(GROUP, FF_AHEAD):
             load_ff(i)
-
+            if i - 1 < RES_AHEAD:
+                load_res(i - 1)
+        for i in range(FF_AHEAD - 1, RES_AHEAD):
+            load_res(i)
         bias_bc = const.tile([P, H], BF16)
-        for h in range(HALVES):
-            bias_ps = psum_acc.tile([P, BANK], F32, name="acc")
-            spread_row("bias", h, bias_ps[:])
-            nc.scalar.copy(out=bias_bc[:, half(h)], in_=bias_ps[:])
-        add_bias(0)
-
-        w_grp = weights.tile([P, PASSES, H, PACK], BF16, align_bytes=64)
-        w_codes = weights.tile([P, PASSES, H], U32, align_bytes=64)
-        w_scales = weights.tile([P, PASSES, H], U8, align_bytes=64)
+        def spread_bias():
+            for h in range(HALVES):
+                bias_ps = psum_acc.tile([P, BANK], F32, name="acc")
+                spread_row("bias", h, bias_ps[:])
+                nc.scalar.copy(out=bias_bc[:, half(h)], in_=bias_ps[:])
 
         def regroup_w(g, h):
-            nc.vector.tensor_copy(
-                out=w_grp[:, g, half(h), :].rearrange("p (c i) t -> p c t i", i=4),
-                in_=w_raw[:, g, :, half(h)].rearrange("p t (c i) -> p c t i", i=4),
-            )
+            dst = w_grp[g, h][:].rearrange("p (c i) t -> p c t i", i=4)
+            src = w_raw[g, h][:].rearrange("p t (c i) -> p c t i", i=4)
+            if (g, h) in SREG:
+                nc.scalar.copy(out=dst, in_=src)
+            else:
+                nc.vector.tensor_copy(out=dst, in_=src)
 
         def quantise_w(g, h):
             nc.vector.quantize_mx(
-                out=w_codes[:, g, half(h)].bitcast(FP8X4),
-                scales=w_scales[:, g, half(h)],
-                in_=w_grp[:, g, half(h), :].rearrange("p n t -> p (n t)"),
+                out=w_codes[g, h][:].bitcast(FP8X4),
+                scales=w_scales[g, h][:],
+                in_=w_grp[g, h][:].rearrange("p n t -> p (n t)"),
             )
-
-        for h in range(HALVES):
-            for g in range(PASSES):
-                regroup_w(g, h)
-            for g in range(PASSES):
-                quantise_w(g, h)
-
-        for i in range(GROUP):
-            transpose(i)
-            regroup(i)
-        quantise_ff(0)
 
         gain_ps = psum_const.tile([P, H], BF16)
         shift_ps = psum_const.tile([P, H], BF16)
-        for h in range(HALVES):
-            spread_row("gain", h, gain_ps[:, half(h)])
-            spread_row("shift", h, shift_ps[:, half(h)])
         shift_bc = const.tile([P, H], BF16)
-        nc.scalar.copy(out=shift_bc[:], in_=shift_ps[:])
 
-        for i in range(GROUP, PREP):
+        transpose(0)
+        regroup(0)
+        regroup_w(0, 0)
+        quantise_w(0, 0)
+        regroup_w(0, 1)
+        regroup_w(1, 0)
+        quantise_w(1, 0)
+        quantise_ff(0, 0, 1)
+        regroup_w(1, 1)
+        quantise_w(0, 1)
+        quantise_w(1, 1)
+        for i in range(1, HEAD_T):
             transpose(i)
             regroup(i)
-
+        add_bias(0)
+        spread_bias()
+        for i in range(1, RB_AHEAD):
+            add_bias(i)
+        def spread_rest():
+            for h in range(HALVES):
+                spread_row("gain", h, gain_ps[:, half(h)])
+                spread_row("shift", h, shift_ps[:, half(h)])
+            nc.scalar.copy(out=shift_bc[:], in_=shift_ps[:])
         def tile_exists(i):
             return 0 <= i < N_TILES
 
-        def handed_over(i):
-            return tile_exists(i) and i % HAND_OVER == 1
+        def prepared(i):
+            return min(N_TILES, HEAD_T + 2 * i, i + PREP)
 
-        for i in range(N_TILES + 4):
+        for i in range(N_TILES + SHIFT_LAG):
             if tile_exists(i + FF_AHEAD):
                 load_ff(i + FF_AHEAD)
             if tile_exists(i + RES_AHEAD):
                 load_res(i + RES_AHEAD)
-            if tile_exists(i + 1):
-                add_bias(i + 1)
+            if tile_exists(i + RB_AHEAD) and not by_tensor(i + RB_AHEAD):
+                add_bias(i + RB_AHEAD)
             if tile_exists(i):
                 project(i)
-            if tile_exists(i + PREP):
-                transpose(i + PREP)
-                regroup(i + PREP)
-            if handed_over(i - 3):
-                scale_only(i - 3)
-            if tile_exists(i):
-                add_residual(i, 0)
-            if tile_exists(i - 2):
-                centre_and_gain(i - 2)
-            if tile_exists(i):
-                add_residual(i, 1)
-                mean(i)
-            if tile_exists(i - 1):
-                inverse_deviation(i - 1)
-            if tile_exists(i):
-                squared_deviations(i)
-            if tile_exists(i - 3) and not handed_over(i - 3):
-                scale_and_shift(i - 3)
-                store(i - 3)
-            if handed_over(i - 4):
-                shift_only(i - 4)
-                store(i - 4)
-            if i % GROUP == GROUP - 2 and tile_exists(i + 2):
-                quantise_ff((i + 2) // GROUP)
+            for t in range(prepared(i), prepared(i + 1)):
+                transpose(t)
+                regroup(t)
+            if i == 0:
+                spread_rest()
+            if tile_exists(i + RB_AHEAD) and by_tensor(i + RB_AHEAD):
+                add_bias(i + RB_AHEAD)
+            if handed_over(i - G2_LAG):
+                scale_only(i - G2_LAG)
+            for what in ORDER.split(' '):
+                if what == 'd0' and tile_exists(i):
+                    add_residual(i, 0)
+                if what == 'g1' and tile_exists(i - G1_LAG):
+                    centre_and_gain(i - G1_LAG)
+                if what == 'd1' and tile_exists(i):
+                    add_residual(i, 1)
+                    mean(i)
+                if what == 'q':
+                    if i == 0:
+                        quantise_ff(0, 1, 2)
+                    elif i == 1:
+                        quantise_ff(0, 2, 4)
+                    elif i % GROUP == GROUP - QLEAD and tile_exists(i + QLEAD):
+                        quantise_ff((i + QLEAD) // GROUP, 0, GROUP)
+                if what == 'g2':
+                    if tile_exists(i - 1):
+                        inverse_deviation(i - 1)
+                    if tile_exists(i):
+                        squared_deviations(i)
+                    if tile_exists(i - G2_LAG) and not handed_over(i - G2_LAG):
+                        scale_and_shift(i - G2_LAG)
+                        store(i - G2_LAG)
+            if handed_over(i - SHIFT_LAG):
+                shift_only(i - SHIFT_LAG)
+                store(i - SHIFT_LAG)

@@ -34,7 +34,6 @@ SHIFT_LAG = 3
 GSPLIT = 1
 SREG = ((0, 1),)
 HEAD_T = 2
-def handed_over(i): return 0 <= i < N_TILES - 1 and i % 8 in (1,3,4,6,7)
 def by_tensor(i): return i % 3 == 0 and i < 33
 def sum_on_vector(i): return True
 def qplace(i): return 'mid'
@@ -42,7 +41,8 @@ ORDER = 'd0 d1 g1 q g2'
 ORDER = 'q d0 d1 g1 g2'
 RB_AHEAD = 3
 RES_AHEAD = RB_AHEAD + 3
-GSPLIT = 2
+GSPLIT = 1
+def handed_over(i): return 0 <= i < N_TILES - 1 and i % 5 in (1, 3)
 
 
 def tile_disentangledattention_pc_t_kernel(tc, ff, attn_out, Wf, b_f, ln2_g, ln2_b, out):

@@ -26,23 +26,24 @@ FLOPS = 2 * TOKENS * K * H
 QLEAD = 1
 PREP = GROUP + 1
 FF_AHEAD = PREP + 3
-RB_AHEAD = 2
-RES_AHEAD = RB_AHEAD + 3
 G1_LAG = 1
 G2_LAG = 2
-SHIFT_LAG = 3
-GSPLIT = 1
 SREG = ((0, 1),)
 HEAD_T = 2
-def by_tensor(i): return i % 3 == 0 and i < 33
 def sum_on_vector(i): return True
 def qplace(i): return 'mid'
-ORDER = 'd0 d1 g1 q g2'
+BT = True
+REST_AT = 0
+CP = True
+ACC = 4
+XT = 2
 ORDER = 'q d0 d1 g1 g2'
-RB_AHEAD = 3
+SHIFT_LAG = 4
+RB_AHEAD = 1
 RES_AHEAD = RB_AHEAD + 3
-GSPLIT = 1
-def handed_over(i): return 0 <= i < N_TILES - 1 and i % 5 in (1, 3)
+GSPLIT = 2
+def handed_over(i): return 0 <= i < N_TILES - 1 and i % 2 == 1
+def by_tensor(i): return i % 2 == 1 and i < N_TILES
 
 
 def tile_disentangledattention_pc_t_kernel(tc, ff, attn_out, Wf, b_f, ln2_g, ln2_b, out):
@@ -62,8 +63,9 @@ def tile_disentangledattention_pc_t_kernel(tc, ff, attn_out, Wf, b_f, ln2_g, ln2
         y_pool = ctx.enter_context(tc.tile_pool(name="y_pool", bufs=6))
         stats = ctx.enter_context(tc.tile_pool(name="stats", bufs=4))
         psum_const = ctx.enter_context(tc.psum_pool(name="psum_const", bufs=1))
-        psum_t = ctx.enter_context(tc.psum_pool(name="psum_t", bufs=2))
-        psum_acc = ctx.enter_context(tc.psum_pool(name="psum_acc", bufs=4))
+        gain_bc = const.tile([P, H], BF16)
+        psum_t = ctx.enter_context(tc.psum_pool(name="psum_t", bufs=XT))
+        psum_acc = ctx.enter_context(tc.psum_pool(name="psum_acc", bufs=ACC))
         ctx.enter_context(tc.manual_schedule())
 
         def half(h):
@@ -113,7 +115,18 @@ def tile_disentangledattention_pc_t_kernel(tc, ff, attn_out, Wf, b_f, ln2_g, ln2
                 for h in range(HALVES):
                     ps = psum_acc.tile([P, BANK], F32, name="acc")
                     nc.tensor.matmul(out=ps[:], lhsT=ident_bf[:], rhs=res_sb[i][:, half(h)], start=True, stop=False)
-                    nc.tensor.matmul(out=ps[:], lhsT=ones[:], rhs=rows["bias"][:, half(h)], start=False, stop=True)
+                    if not BT:
+                        nc.tensor.matmul(out=ps[:], lhsT=ones[:], rhs=rows["bias"][:, half(h)], start=False, stop=True)
+                    for c in range(BANK // P if BT else 0):
+                        k = h * (BANK // P) + c
+                        nc.tensor.matmul(
+                            out=ps[:, c * P : (c + 1) * P],
+                            lhsT=bias_col[:, k : k + 1].to_broadcast([P, P]),
+                            rhs=ident[:],
+                            is_transpose=True,
+                            start=False,
+                            stop=(c == BANK // P - 1),
+                        )
                     nc.scalar.copy(out=rb[i][:, half(h)], in_=ps[:])
                 return
             w = H // GSPLIT
@@ -166,10 +179,10 @@ def tile_disentangledattention_pc_t_kernel(tc, ff, attn_out, Wf, b_f, ln2_g, ln2
 
         def centre_and_gain(i):
             y[i] = y_pool.tile([P, H], F32, name="y")
-            nc.vector.scalar_tensor_tensor(out=y[i][:], in0=u[i][:], scalar=negmean[i][:], in1=gain_ps[:], op0=ALU.add, op1=ALU.mult)
+            nc.vector.scalar_tensor_tensor(out=y[i][:], in0=u[i][:], scalar=negmean[i][:], in1=vgain[0][:], op0=ALU.add, op1=ALU.mult)
 
         def scale_and_shift(i):
-            nc.vector.scalar_tensor_tensor(out=y[i][:], in0=y[i][:], scalar=rstd[i][:], in1=shift_ps[:], op0=ALU.mult, op1=ALU.add)
+            nc.vector.scalar_tensor_tensor(out=y[i][:], in0=y[i][:], scalar=rstd[i][:], in1=vgain[1][:], op0=ALU.mult, op1=ALU.add)
 
         def scale_only(i):
             nc.scalar.activation(out=y[i][:], in_=y[i][:], func=ACT.Copy, scale=rstd[i][:])
@@ -215,32 +228,35 @@ def tile_disentangledattention_pc_t_kernel(tc, ff, attn_out, Wf, b_f, ln2_g, ln2
         def load_w(g, h):
             nc.sync.dma_start(out=w_raw[g, h][:], in_=w_v[g][:, :, half(h)])
 
+        load_row("bias", b_f)
         load_w(0, 0)
         load_ff(0)
         load_w(1, 0)
-        load_w(0, 1)
-        load_w(1, 1)
         load_res(0)
-        load_row("bias", b_f)
+        load_w(0, 1)
         load_ff(1)
-        load_res(1)
+        load_w(1, 1)
         load_ff(2)
         load_ff(3)
-        load_res(2)
         load_row("gain", ln2_g)
         load_row("shift", ln2_b)
-        for i in range(GROUP, FF_AHEAD):
-            load_ff(i)
-            if i - 1 < RES_AHEAD:
-                load_res(i - 1)
-        for i in range(FF_AHEAD - 1, RES_AHEAD):
+        for i in range(1, RES_AHEAD):
             load_res(i)
+            if GROUP - 1 + i < FF_AHEAD:
+                load_ff(GROUP - 1 + i)
+        for i in range(GROUP - 1 + RES_AHEAD, FF_AHEAD):
+            load_ff(i)
         bias_bc = const.tile([P, H], BF16)
+        bias_col = const.tile([P, H // P], F32)
         def spread_bias():
             for h in range(HALVES):
                 bias_ps = psum_acc.tile([P, BANK], F32, name="acc")
                 spread_row("bias", h, bias_ps[:])
                 nc.scalar.copy(out=bias_bc[:, half(h)], in_=bias_ps[:])
+            turned = psum_t.tile([P, H // P, P], BF16, name="xt")
+            for c in range(H // P):
+                nc.tensor.transpose(turned[:, c, :], bias_bc[:, c * P : (c + 1) * P], ident_bf[:])
+            nc.scalar.copy(out=bias_col[:], in_=turned[:, :, 0])
 
         def regroup_w(g, h):
             dst = w_grp[g, h][:].rearrange("p (c i) t -> p c t i", i=4)
@@ -257,10 +273,15 @@ def tile_disentangledattention_pc_t_kernel(tc, ff, attn_out, Wf, b_f, ln2_g, ln2
                 in_=w_grp[g, h][:].rearrange("p n t -> p (n t)"),
             )
 
-        gain_ps = psum_const.tile([P, H], BF16)
-        shift_ps = psum_const.tile([P, H], BF16)
         shift_bc = const.tile([P, H], BF16)
+        if CP:
+            gain_ps = psum_const.tile([P, H], BF16)
+            shift_ps = psum_const.tile([P, H], BF16)
+            vgain = (gain_ps, shift_ps)
+        else:
+            vgain = (gain_bc, shift_bc)
 
+        spread_bias()
         transpose(0)
         regroup(0)
         regroup_w(0, 0)
@@ -272,18 +293,24 @@ def tile_disentangledattention_pc_t_kernel(tc, ff, attn_out, Wf, b_f, ln2_g, ln2
         regroup_w(1, 1)
         quantise_w(0, 1)
         quantise_w(1, 1)
+        add_bias(0)
         for i in range(1, HEAD_T):
             transpose(i)
             regroup(i)
-        add_bias(0)
-        spread_bias()
         for i in range(1, RB_AHEAD):
             add_bias(i)
         def spread_rest():
-            for h in range(HALVES):
-                spread_row("gain", h, gain_ps[:, half(h)])
-                spread_row("shift", h, shift_ps[:, half(h)])
-            nc.scalar.copy(out=shift_bc[:], in_=shift_ps[:])
+            if CP:
+                for h in range(HALVES):
+                    spread_row("gain", h, gain_ps[:, half(h)])
+                    spread_row("shift", h, shift_ps[:, half(h)])
+                nc.scalar.copy(out=shift_bc[:], in_=shift_ps[:])
+            else:
+                for name, dst in (("gain", gain_bc), ("shift", shift_bc)):
+                    tp2 = psum_t.tile([P, H], BF16, name="xt")
+                    for h in range(HALVES):
+                        spread_row(name, h, tp2[:, half(h)])
+                    nc.scalar.copy(out=dst[:], in_=tp2[:])
         def tile_exists(i):
             return 0 <= i < N_TILES
 
@@ -302,7 +329,7 @@ def tile_disentangledattention_pc_t_kernel(tc, ff, attn_out, Wf, b_f, ln2_g, ln2
             for t in range(prepared(i), prepared(i + 1)):
                 transpose(t)
                 regroup(t)
-            if i == 0:
+            if i == REST_AT:
                 spread_rest()
             if tile_exists(i + RB_AHEAD) and by_tensor(i + RB_AHEAD):
                 add_bias(i + RB_AHEAD)

@@ -28,22 +28,22 @@ PREP = GROUP + 1
 FF_AHEAD = PREP + 3
 G1_LAG = 1
 G2_LAG = 2
+SHIFT_LAG = 3
+GSPLIT = 1
 SREG = ((0, 1),)
 HEAD_T = 2
-def sum_on_vector(i): return True
 def qplace(i): return 'mid'
 BT = True
 REST_AT = 0
 CP = True
 ACC = 4
 XT = 2
-ORDER = 'q d0 d1 g1 g2'
-SHIFT_LAG = 4
 RB_AHEAD = 1
 RES_AHEAD = RB_AHEAD + 3
-GSPLIT = 2
-def handed_over(i): return 0 <= i < N_TILES - 1 and i % 2 == 1
-def by_tensor(i): return i % 2 == 1 and i < N_TILES
+ORDER = 'q d0 d1 g1 g2'
+def handed_over(i): return 0 <= i < N_TILES - 1 and i % 2 == 0
+def by_tensor(i): return i % 2 == 0 and i < N_TILES
+def sum_on_vector(i): return i % 4 != 0
 
 
 def tile_disentangledattention_pc_t_kernel(tc, ff, attn_out, Wf, b_f, ln2_g, ln2_b, out):
@@ -121,7 +121,7 @@ def tile_disentangledattention_pc_t_kernel(tc, ff, attn_out, Wf, b_f, ln2_g, ln2
                         k = h * (BANK // P) + c
                         nc.tensor.matmul(
                             out=ps[:, c * P : (c + 1) * P],
-                            lhsT=bias_col[:, k : k + 1].to_broadcast([P, P]),
+                            lhsT=bias_turned[:, k, :],
                             rhs=ident[:],
                             is_transpose=True,
                             start=False,
@@ -247,7 +247,7 @@ def tile_disentangledattention_pc_t_kernel(tc, ff, attn_out, Wf, b_f, ln2_g, ln2
         for i in range(GROUP - 1 + RES_AHEAD, FF_AHEAD):
             load_ff(i)
         bias_bc = const.tile([P, H], BF16)
-        bias_col = const.tile([P, H // P], F32)
+        bias_turned = const.tile([P, H // P, P], F32)
         def spread_bias():
             for h in range(HALVES):
                 bias_ps = psum_acc.tile([P, BANK], F32, name="acc")
@@ -256,7 +256,7 @@ def tile_disentangledattention_pc_t_kernel(tc, ff, attn_out, Wf, b_f, ln2_g, ln2
             turned = psum_t.tile([P, H // P, P], BF16, name="xt")
             for c in range(H // P):
                 nc.tensor.transpose(turned[:, c, :], bias_bc[:, c * P : (c + 1) * P], ident_bf[:])
-            nc.scalar.copy(out=bias_col[:], in_=turned[:, :, 0])
+            nc.scalar.copy(out=bias_turned[:], in_=turned[:])
 
         def regroup_w(g, h):
             dst = w_grp[g, h][:].rearrange("p (c i) t -> p c t i", i=4)

@@ -28,22 +28,22 @@ PREP = GROUP + 1
 FF_AHEAD = PREP + 3
 G1_LAG = 1
 G2_LAG = 2
-SHIFT_LAG = 3
 GSPLIT = 1
 SREG = ((0, 1),)
 HEAD_T = 2
+def sum_on_vector(i): return True
 def qplace(i): return 'mid'
 BT = True
 REST_AT = 0
 CP = True
 ACC = 4
 XT = 2
+SHIFT_LAG = 4
 RB_AHEAD = 1
 RES_AHEAD = RB_AHEAD + 3
-ORDER = 'q d0 d1 g1 g2'
+ORDER = 'd0 d1 q g1 g2'
 def handed_over(i): return 0 <= i < N_TILES - 1 and i % 2 == 0
 def by_tensor(i): return i % 2 == 0 and i < N_TILES
-def sum_on_vector(i): return i % 4 != 0
 
 
 def tile_disentangledattention_pc_t_kernel(tc, ff, attn_out, Wf, b_f, ln2_g, ln2_b, out):

@@ -29,21 +29,30 @@ FF_AHEAD = PREP + 3
 G1_LAG = 1
 G2_LAG = 2
 GSPLIT = 1
-SREG = ((0, 1),)
 HEAD_T = 2
 def sum_on_vector(i): return True
 def qplace(i): return 'mid'
 BT = True
-REST_AT = 0
+Q23 = 1
+RE = True
+BF = True
+ONES = (0,)
 CP = True
 ACC = 4
 XT = 2
+TB_AT = 99
+REST_AT = 99
+FIRST2 = False
+SREG = ()
+ORDER = 'q d0 d1 g1 g2'
+GAIN_LAG = 3
 SHIFT_LAG = 4
 RB_AHEAD = 1
-RES_AHEAD = RB_AHEAD + 3
-ORDER = 'd0 d1 q g1 g2'
-def handed_over(i): return 0 <= i < N_TILES - 1 and i % 2 == 0
-def by_tensor(i): return i % 2 == 0 and i < N_TILES
+RES_AHEAD = 4
+HEADSEQ = 'S R t0 r00 q00 t1 T r10 q10 f02 r01 r11 q01 q11 b0 p00 t2 p01'
+def full(i): return 0 <= i < N_TILES - 2 and i % 8 in (0, 3)
+def handed_over(i): return 0 <= i < N_TILES - 1 and i % 8 == 5
+def by_tensor(i): return 0 <= i < N_TILES and (i % 2 == 0 or i % 8 == 7)
 
 
 def tile_disentangledattention_pc_t_kernel(tc, ff, attn_out, Wf, b_f, ln2_g, ln2_b, out):
@@ -115,9 +124,9 @@ def tile_disentangledattention_pc_t_kernel(tc, ff, attn_out, Wf, b_f, ln2_g, ln2
                 for h in range(HALVES):
                     ps = psum_acc.tile([P, BANK], F32, name="acc")
                     nc.tensor.matmul(out=ps[:], lhsT=ident_bf[:], rhs=res_sb[i][:, half(h)], start=True, stop=False)
-                    if not BT:
+                    if not BT or i in ONES:
                         nc.tensor.matmul(out=ps[:], lhsT=ones[:], rhs=rows["bias"][:, half(h)], start=False, stop=True)
-                    for c in range(BANK // P if BT else 0):
+                    for c in range(BANK // P if BT and i not in ONES else 0):
                         k = h * (BANK // P) + c
                         nc.tensor.matmul(
                             out=ps[:, c * P : (c + 1) * P],
@@ -134,9 +143,9 @@ def tile_disentangledattention_pc_t_kernel(tc, ff, attn_out, Wf, b_f, ln2_g, ln2
                 c = slice(s * w, s * w + w)
                 nc.gpsimd.tensor_tensor(out=rb[i][:, c], in0=res_sb[i][:, c], in1=bias_bc[:, c], op=ALU.add)
 
-        def project(i):
+        def project(i, halves=range(HALVES)):
             ff_codes, ff_scales = codes[i // GROUP]
-            for h in range(HALVES):
+            for h in halves:
                 acc[i, h] = psum_acc.tile([P, BANK], F32, name="acc")
                 for g in range(PASSES):
                     tok = slice(((i % GROUP) * PASSES + g) * P, ((i % GROUP) * PASSES + g + 1) * P)
@@ -180,6 +189,22 @@ def tile_disentangledattention_pc_t_kernel(tc, ff, attn_out, Wf, b_f, ln2_g, ln2
         def centre_and_gain(i):
             y[i] = y_pool.tile([P, H], F32, name="y")
             nc.vector.scalar_tensor_tensor(out=y[i][:], in0=u[i][:], scalar=negmean[i][:], in1=vgain[0][:], op0=ALU.add, op1=ALU.mult)
+
+        nmr = {}
+
+        def centre(i):
+            nmr[i] = stats.tile([P, 1], F32, name="nmr")
+            nc.scalar.activation(out=nmr[i][:], in_=negmean[i][:], func=ACT.Copy, scale=rstd[i][:])
+
+        def normalise(i):
+            y[i] = y_pool.tile([P, H], F32, name="y")
+            nc.scalar.activation(out=y[i][:], in_=u[i][:], func=ACT.Identity, scale=rstd[i][:], bias=nmr[i][:])
+
+        def gain_only(i):
+            w = H // GSPLIT
+            for s in range(GSPLIT):
+                c = slice(s * w, s * w + w)
+                nc.gpsimd.tensor_tensor(out=y[i][:, c], in0=y[i][:, c], in1=gain_bc[:, c], op=ALU.mult)
 
         def scale_and_shift(i):
             nc.vector.scalar_tensor_tensor(out=y[i][:], in0=y[i][:], scalar=rstd[i][:], in1=vgain[1][:], op0=ALU.mult, op1=ALU.add)
@@ -225,21 +250,41 @@ def tile_disentangledattention_pc_t_kernel(tc, ff, attn_out, Wf, b_f, ln2_g, ln2
                 w_codes[g, h] = weights.tile([P, BANK], U32, align_bytes=64, name="w_codes%d%d" % (g, h))
                 w_scales[g, h] = weights.tile([P, BANK], U8, align_bytes=64, name="w_scales%d%d" % (g, h))
 
-        def load_w(g, h):
-            nc.sync.dma_start(out=w_raw[g, h][:], in_=w_v[g][:, :, half(h)])
+        def load_w(g, h, part=None):
+            if part is None:
+                nc.sync.dma_start(out=w_raw[g, h][:], in_=w_v[g][:, :, half(h)])
+            else:
+                lo = h * BANK + part * (BANK // 2)
+                nc.sync.dma_start(out=w_parts[part][:], in_=w_v[g][:, :, lo : lo + BANK // 2])
 
-        load_row("bias", b_f)
-        load_w(0, 0)
+        if FIRST2:
+            w_parts = {}
+            for part in range(2):
+                w_parts[part] = weights.tile([P, PACK, BANK // 2], BF16, name="w_part%d" % part)
+            load_w(0, 0, 0)
+            if BF:
+                load_row("bias", b_f)
+            load_w(0, 0, 1)
+        else:
+            load_w(0, 0)
+            if BF:
+                load_row("bias", b_f)
+            if RE:
+                load_row("gain", ln2_g)
+                load_row("shift", ln2_b)
         load_ff(0)
         load_w(1, 0)
-        load_res(0)
-        load_w(0, 1)
         load_ff(1)
+        load_res(0)
+        if not BF:
+            load_row("bias", b_f)
+        load_w(0, 1)
         load_w(1, 1)
         load_ff(2)
         load_ff(3)
-        load_row("gain", ln2_g)
-        load_row("shift", ln2_b)
+        if not RE:
+            load_row("gain", ln2_g)
+            load_row("shift", ln2_b)
         for i in range(1, RES_AHEAD):
             load_res(i)
             if GROUP - 1 + i < FF_AHEAD:
@@ -253,12 +298,20 @@ def tile_disentangledattention_pc_t_kernel(tc, ff, attn_out, Wf, b_f, ln2_g, ln2
                 bias_ps = psum_acc.tile([P, BANK], F32, name="acc")
                 spread_row("bias", h, bias_ps[:])
                 nc.scalar.copy(out=bias_bc[:, half(h)], in_=bias_ps[:])
+        def turn_bias():
             turned = psum_t.tile([P, H // P, P], BF16, name="xt")
             for c in range(H // P):
                 nc.tensor.transpose(turned[:, c, :], bias_bc[:, c * P : (c + 1) * P], ident_bf[:])
             nc.scalar.copy(out=bias_turned[:], in_=turned[:])
 
         def regroup_w(g, h):
+            if FIRST2 and (g, h) == (0, 0):
+                for part in range(2):
+                    nc.vector.tensor_copy(
+                        out=w_grp[g, h][:, part * (BANK // 2) : (part + 1) * (BANK // 2), :].rearrange("p (c i) t -> p c t i", i=4),
+                        in_=w_parts[part][:].rearrange("p t (c i) -> p c t i", i=4),
+                    )
+                return
             dst = w_grp[g, h][:].rearrange("p (c i) t -> p c t i", i=4)
             src = w_raw[g, h][:].rearrange("p t (c i) -> p c t i", i=4)
             if (g, h) in SREG:
@@ -281,72 +334,83 @@ def tile_disentangledattention_pc_t_kernel(tc, ff, attn_out, Wf, b_f, ln2_g, ln2
         else:
             vgain = (gain_bc, shift_bc)
 
-        spread_bias()
-        transpose(0)
-        regroup(0)
-        regroup_w(0, 0)
-        quantise_w(0, 0)
-        regroup_w(0, 1)
-        regroup_w(1, 0)
-        quantise_w(1, 0)
-        quantise_ff(0, 0, 1)
-        regroup_w(1, 1)
-        quantise_w(0, 1)
-        quantise_w(1, 1)
-        add_bias(0)
-        for i in range(1, HEAD_T):
-            transpose(i)
-            regroup(i)
-        for i in range(1, RB_AHEAD):
-            add_bias(i)
         def spread_rest():
             if CP:
                 for h in range(HALVES):
                     spread_row("gain", h, gain_ps[:, half(h)])
                     spread_row("shift", h, shift_ps[:, half(h)])
                 nc.scalar.copy(out=shift_bc[:], in_=shift_ps[:])
+                nc.scalar.copy(out=gain_bc[:], in_=gain_ps[:])
             else:
                 for name, dst in (("gain", gain_bc), ("shift", shift_bc)):
                     tp2 = psum_t.tile([P, H], BF16, name="xt")
                     for h in range(HALVES):
                         spread_row(name, h, tp2[:, half(h)])
                     nc.scalar.copy(out=dst[:], in_=tp2[:])
+        done_first = set()
+        for op in HEADSEQ.split():
+            a = op[1:]
+            if op[0] == "t":
+                transpose(int(a))
+                regroup(int(a))
+                head_turned = int(a) + 1
+            elif op[0] == "r":
+                regroup_w(int(a[0]), int(a[1]))
+            elif op[0] == "q":
+                quantise_w(int(a[0]), int(a[1]))
+            elif op[0] == "f":
+                quantise_ff(0, int(a[0]), int(a[1]))
+            elif op[0] == "b":
+                add_bias(int(a))
+            elif op[0] == "p":
+                project(int(a[0]), (int(a[1]),))
+                done_first.add((int(a[0]), int(a[1])))
+            elif op == "S":
+                spread_bias()
+            elif op == "R":
+                spread_rest()
+            elif op == "T":
+                turn_bias()
         def tile_exists(i):
             return 0 <= i < N_TILES
 
         def prepared(i):
-            return min(N_TILES, HEAD_T + 2 * i, i + PREP)
+            return min(N_TILES, head_turned + 2 * i, i + PREP)
 
         for i in range(N_TILES + SHIFT_LAG):
             if tile_exists(i + FF_AHEAD):
                 load_ff(i + FF_AHEAD)
             if tile_exists(i + RES_AHEAD):
                 load_res(i + RES_AHEAD)
-            if tile_exists(i + RB_AHEAD) and not by_tensor(i + RB_AHEAD):
+            if tile_exists(i + RB_AHEAD) and not by_tensor(i + RB_AHEAD) and i + RB_AHEAD not in rb:
                 add_bias(i + RB_AHEAD)
             if tile_exists(i):
-                project(i)
+                left = tuple(h for h in range(HALVES) if (i, h) not in done_first)
+                if left:
+                    project(i, left)
             for t in range(prepared(i), prepared(i + 1)):
                 transpose(t)
                 regroup(t)
             if i == REST_AT:
                 spread_rest()
-            if tile_exists(i + RB_AHEAD) and by_tensor(i + RB_AHEAD):
+            if i == TB_AT:
+                turn_bias()
+            if tile_exists(i + RB_AHEAD) and by_tensor(i + RB_AHEAD) and i + RB_AHEAD not in rb:
                 add_bias(i + RB_AHEAD)
-            if handed_over(i - G2_LAG):
+            if full(i - G2_LAG):
+                normalise(i - G2_LAG)
+            elif handed_over(i - G2_LAG):
                 scale_only(i - G2_LAG)
             for what in ORDER.split(' '):
                 if what == 'd0' and tile_exists(i):
                     add_residual(i, 0)
-                if what == 'g1' and tile_exists(i - G1_LAG):
+                if what == 'g1' and tile_exists(i - G1_LAG) and not full(i - G1_LAG):
                     centre_and_gain(i - G1_LAG)
                 if what == 'd1' and tile_exists(i):
                     add_residual(i, 1)
                     mean(i)
                 if what == 'q':
-                    if i == 0:
-                        quantise_ff(0, 1, 2)
-                    elif i == 1:
+                    if i == Q23:
                         quantise_ff(0, 2, 4)
                     elif i % GROUP == GROUP - QLEAD and tile_exists(i + QLEAD):
                         quantise_ff((i + QLEAD) // GROUP, 0, GROUP)
@@ -355,9 +419,13 @@ def tile_disentangledattention_pc_t_kernel(tc, ff, attn_out, Wf, b_f, ln2_g, ln2
                         inverse_deviation(i - 1)
                     if tile_exists(i):
                         squared_deviations(i)
-                    if tile_exists(i - G2_LAG) and not handed_over(i - G2_LAG):
+                    if full(i - 1):
+                        centre(i - 1)
+                    if tile_exists(i - G2_LAG) and not handed_over(i - G2_LAG) and not full(i - G2_LAG):
                         scale_and_shift(i - G2_LAG)
                         store(i - G2_LAG)
-            if handed_over(i - SHIFT_LAG):
+            if full(i - GAIN_LAG):
+                gain_only(i - GAIN_LAG)
+            if handed_over(i - SHIFT_LAG) or full(i - SHIFT_LAG):
                 shift_only(i - SHIFT_LAG)
                 store(i - SHIFT_LAG)

@@ -33,7 +33,7 @@ HEAD_T = 2
 def sum_on_vector(i): return True
 def qplace(i): return 'mid'
 BT = True
-Q23 = 1
+VCW = 'g2'
 RE = True
 BF = True
 ONES = (0,)
@@ -42,6 +42,7 @@ ACC = 4
 XT = 2
 TB_AT = 99
 REST_AT = 99
+Q23 = 99
 FIRST2 = False
 SREG = ()
 ORDER = 'q d0 d1 g1 g2'
@@ -49,7 +50,8 @@ GAIN_LAG = 3
 SHIFT_LAG = 4
 RB_AHEAD = 1
 RES_AHEAD = 4
-HEADSEQ = 'S R t0 r00 q00 t1 T r10 q10 f02 r01 r11 q01 q11 b0 p00 t2 p01'
+VC = (0, 1, 2)
+HEADSEQ = 'S t0 r00 q00 t1 R r10 q10 b0 f02 r01 r11 q01 q11 T t2 p00 t3 b1 f24 p01'
 def full(i): return 0 <= i < N_TILES - 2 and i % 8 in (0, 3)
 def handed_over(i): return 0 <= i < N_TILES - 1 and i % 8 == 5
 def by_tensor(i): return 0 <= i < N_TILES and (i % 2 == 0 or i % 8 == 7)
@@ -120,6 +122,9 @@ def tile_disentangledattention_pc_t_kernel(tc, ff, attn_out, Wf, b_f, ln2_g, ln2
 
         def add_bias(i):
             rb[i] = rb_pool.tile([P, H], F32, name="rb")
+            if i in VC:
+                nc.vector.tensor_tensor(out=rb[i][:], in0=res_sb[i][:], in1=bias_bc[:], op=ALU.add)
+                return
             if by_tensor(i):
                 for h in range(HALVES):
                     ps = psum_acc.tile([P, BANK], F32, name="acc")
@@ -348,6 +353,7 @@ def tile_disentangledattention_pc_t_kernel(tc, ff, attn_out, Wf, b_f, ln2_g, ln2
                         spread_row(name, h, tp2[:, half(h)])
                     nc.scalar.copy(out=dst[:], in_=tp2[:])
         done_first = set()
+        done_d = set()
         for op in HEADSEQ.split():
             a = op[1:]
             if op[0] == "t":
@@ -362,6 +368,11 @@ def tile_disentangledattention_pc_t_kernel(tc, ff, attn_out, Wf, b_f, ln2_g, ln2
                 quantise_ff(0, int(a[0]), int(a[1]))
             elif op[0] == "b":
                 add_bias(int(a))
+            elif op[0] == "d":
+                add_residual(int(a[0]), int(a[1]))
+                done_d.add((int(a[0]), int(a[1])))
+                if a[1] == "1":
+                    mean(int(a[0]))
             elif op[0] == "p":
                 project(int(a[0]), (int(a[1]),))
                 done_first.add((int(a[0]), int(a[1])))
@@ -382,7 +393,7 @@ def tile_disentangledattention_pc_t_kernel(tc, ff, attn_out, Wf, b_f, ln2_g, ln2
                 load_ff(i + FF_AHEAD)
             if tile_exists(i + RES_AHEAD):
                 load_res(i + RES_AHEAD)
-            if tile_exists(i + RB_AHEAD) and not by_tensor(i + RB_AHEAD) and i + RB_AHEAD not in rb:
+            if tile_exists(i + RB_AHEAD) and not by_tensor(i + RB_AHEAD) and i + RB_AHEAD not in rb and i + RB_AHEAD not in VC:
                 add_bias(i + RB_AHEAD)
             if tile_exists(i):
                 left = tuple(h for h in range(HALVES) if (i, h) not in done_first)
@@ -395,18 +406,20 @@ def tile_disentangledattention_pc_t_kernel(tc, ff, attn_out, Wf, b_f, ln2_g, ln2
                 spread_rest()
             if i == TB_AT:
                 turn_bias()
-            if tile_exists(i + RB_AHEAD) and by_tensor(i + RB_AHEAD) and i + RB_AHEAD not in rb:
+            if tile_exists(i + RB_AHEAD) and by_tensor(i + RB_AHEAD) and i + RB_AHEAD not in rb and i + RB_AHEAD not in VC:
                 add_bias(i + RB_AHEAD)
             if full(i - G2_LAG):
                 normalise(i - G2_LAG)
             elif handed_over(i - G2_LAG):
                 scale_only(i - G2_LAG)
             for what in ORDER.split(' '):
-                if what == 'd0' and tile_exists(i):
+                if what == VCW and i + 1 in VC and i + 1 not in rb:
+                    add_bias(i + 1)
+                if what == 'd0' and tile_exists(i) and (i, 0) not in done_d:
                     add_residual(i, 0)
                 if what == 'g1' and tile_exists(i - G1_LAG) and not full(i - G1_LAG):
                     centre_and_gain(i - G1_LAG)
-                if what == 'd1' and tile_exists(i):
+                if what == 'd1' and tile_exists(i) and (i, 1) not in done_d:
                     add_residual(i, 1)
                     mean(i)
                 if what == 'q':

@@ -34,6 +34,10 @@ def sum_on_vector(i): return True
 def qplace(i): return 'mid'
 BT = True
 VCW = 'g2'
+YB = 6
+WB = 4
+STORE_LAST = 28
+ADDPOS = 'start'
 RE = True
 BF = True
 ONES = (0,)
@@ -51,9 +55,10 @@ SHIFT_LAG = 4
 RB_AHEAD = 1
 RES_AHEAD = 4
 VC = (0, 1, 2)
+LASTH = (30, 31)
 HEADSEQ = 'S t0 r00 q00 t1 R r10 q10 b0 f02 r01 r11 q01 q11 T t2 p00 t3 b1 f24 p01'
-def full(i): return 0 <= i < N_TILES - 2 and i % 8 in (0, 3)
-def handed_over(i): return 0 <= i < N_TILES - 1 and i % 8 == 5
+def full(i): return 0 <= i < N_TILES - 2 and i % 4 == 0
+def handed_over(i): return 0 <= i < N_TILES - 1 and i % 8 == 2
 def by_tensor(i): return 0 <= i < N_TILES and (i % 2 == 0 or i % 8 == 7)
 
 
@@ -70,8 +75,8 @@ def tile_disentangledattention_pc_t_kernel(tc, ff, attn_out, Wf, b_f, ln2_g, ln2
         res_pool = ctx.enter_context(tc.tile_pool(name="res_pool", bufs=RES_AHEAD + 1))
         quant = ctx.enter_context(tc.tile_pool(name="quant", bufs=2))
         rb_pool = ctx.enter_context(tc.tile_pool(name="rb_pool", bufs=RB_AHEAD + 1))
-        work = ctx.enter_context(tc.tile_pool(name="work", bufs=4))
-        y_pool = ctx.enter_context(tc.tile_pool(name="y_pool", bufs=6))
+        work = ctx.enter_context(tc.tile_pool(name="work", bufs=WB))
+        y_pool = ctx.enter_context(tc.tile_pool(name="y_pool", bufs=YB))
         stats = ctx.enter_context(tc.tile_pool(name="stats", bufs=4))
         psum_const = ctx.enter_context(tc.psum_pool(name="psum_const", bufs=1))
         gain_bc = const.tile([P, H], BF16)
@@ -434,11 +439,19 @@ def tile_disentangledattention_pc_t_kernel(tc, ff, attn_out, Wf, b_f, ln2_g, ln2
                         squared_deviations(i)
                     if full(i - 1):
                         centre(i - 1)
-                    if tile_exists(i - G2_LAG) and not handed_over(i - G2_LAG) and not full(i - G2_LAG):
-                        scale_and_shift(i - G2_LAG)
-                        store(i - G2_LAG)
+                    t = i - G2_LAG
+                    if t in LASTH:
+                        for h in range(HALVES):
+                            nc.vector.scalar_tensor_tensor(out=y[t][:, half(h)], in0=y[t][:, half(h)], scalar=rstd[t][:], in1=vgain[1][:, half(h)], op0=ALU.mult, op1=ALU.add)
+                            nc.sync.dma_start(out=out_v[t][:, half(h)], in_=y[t][:, half(h)])
+                    elif tile_exists(t) and not handed_over(t) and not full(t):
+                        scale_and_shift(t)
+                        store(t)
             if full(i - GAIN_LAG):
                 gain_only(i - GAIN_LAG)
             if handed_over(i - SHIFT_LAG) or full(i - SHIFT_LAG):
                 shift_only(i - SHIFT_LAG)
-                store(i - SHIFT_LAG)
+                if i - SHIFT_LAG != STORE_LAST:
+                    store(i - SHIFT_LAG)
+        if STORE_LAST >= 0:
+            store(STORE_LAST)

from contextlib import ExitStack

import concourse.mybir as mybir
from concourse.masks import make_identity

F32 = mybir.dt.float32
BF16 = mybir.dt.bfloat16
I32 = mybir.dt.int32
U32 = mybir.dt.uint32
U8 = mybir.dt.uint8
FP8X4 = mybir.dt.float8_e4m3fn_x4
ALU = mybir.AluOpType
ACT = mybir.ActivationFunctionType

P = 128
PACK = 4
K_PASS = P * PACK
TOKENS, K, H = 8 * 512, 1024, 1024
PASSES = K // K_PASS
N_TILES = TOKENS // P
GROUP = 4
BANK = 512
HALVES = H // BANK
EPS = 1e-7
FLOPS = 2 * TOKENS * K * H
QLEAD = 1
PREP = GROUP + 1
FF_AHEAD = PREP + 3
G1_LAG = 1
G2_LAG = 2
GSPLIT = 1
HEAD_T = 2
def sum_on_vector(i): return True
def qplace(i): return 'mid'
BT = True
VCW = 'g2'
YB = 6
WB = 4
STORE_LAST = 28
ADDPOS = 'start'
RE = True
BF = True
ONES = (0,)
CP = True
ACC = 4
XT = 2
TB_AT = 99
REST_AT = 99
Q23 = 99
FIRST2 = False
SREG = ()
ORDER = 'q d0 d1 g1 g2'
GAIN_LAG = 3
SHIFT_LAG = 4
RB_AHEAD = 1
RES_AHEAD = 4
VC = (0, 1, 2)
LASTH = (30, 31)
HEADSEQ = 'S t0 r00 q00 t1 R r10 q10 b0 f02 r01 r11 q01 q11 T t2 p00 t3 b1 f24 p01'
def full(i): return 0 <= i < N_TILES - 2 and i % 4 == 0
def handed_over(i): return 0 <= i < N_TILES - 1 and i % 8 == 2
def by_tensor(i): return 0 <= i < N_TILES and (i % 2 == 0 or i % 8 == 7)


def tile_disentangledattention_pc_t_kernel(tc, ff, attn_out, Wf, b_f, ln2_g, ln2_b, out):
    nc = tc.nc
    ff_v = ff.rearrange("b s f -> (b s) f").rearrange("(i p) f -> i p f", p=P)
    res_v = attn_out.rearrange("b s f -> (b s) f").rearrange("(i p) f -> i p f", p=P)
    out_v = out.rearrange("b s f -> (b s) f").rearrange("(i p) f -> i p f", p=P)
    w_v = Wf.rearrange("(g p t) n -> g p t n", p=P, t=PACK)
    with ExitStack() as ctx:
        const = ctx.enter_context(tc.tile_pool(name="const", bufs=1))
        weights = ctx.enter_context(tc.tile_pool(name="weights", bufs=1))
        ff_pool = ctx.enter_context(tc.tile_pool(name="ff_pool", bufs=FF_AHEAD))
        res_pool = ctx.enter_context(tc.tile_pool(name="res_pool", bufs=RES_AHEAD + 1))
        quant = ctx.enter_context(tc.tile_pool(name="quant", bufs=2))
        rb_pool = ctx.enter_context(tc.tile_pool(name="rb_pool", bufs=RB_AHEAD + 1))
        work = ctx.enter_context(tc.tile_pool(name="work", bufs=WB))
        y_pool = ctx.enter_context(tc.tile_pool(name="y_pool", bufs=YB))
        stats = ctx.enter_context(tc.tile_pool(name="stats", bufs=4))
        psum_const = ctx.enter_context(tc.psum_pool(name="psum_const", bufs=1))
        gain_bc = const.tile([P, H], BF16)
        psum_t = ctx.enter_context(tc.psum_pool(name="psum_t", bufs=XT))
        psum_acc = ctx.enter_context(tc.psum_pool(name="psum_acc", bufs=ACC))
        ctx.enter_context(tc.manual_schedule())

        def half(h):
            return slice(h * BANK, (h + 1) * BANK)

        ff_sb, res_sb, xt, grouped, codes = {}, {}, {}, {}, {}
        rb, acc, u, total, negmean, ssq, rstd, y = {}, {}, {}, {}, {}, {}, {}, {}

        def load_ff(i):
            ff_sb[i] = ff_pool.tile([P, K], BF16, name="ff_sb")
            nc.sync.dma_start(out=ff_sb[i][:], in_=ff_v[i])

        def load_res(i):
            res_sb[i] = res_pool.tile([P, H], BF16, name="res_sb")
            nc.sync.dma_start(out=res_sb[i][:], in_=res_v[i])

        def transpose(i):
            words = ff_sb[i][:].bitcast(F32)
            xt[i] = psum_t.tile([P, PASSES * 2, P], F32, name="xt")
            for g in range(PASSES):
                for u2 in range(2):
                    nc.tensor.transpose(xt[i][:, 2 * g + u2, :], words[:, 2 * P * g + u2 : 2 * P * (g + 1) : 2], ident[:])

        def regroup(i):
            if i % GROUP == 0:
                grouped[i // GROUP] = quant.tile([P, GROUP, PASSES, P, PACK], BF16, align_bytes=64, name="grouped")
            nc.scalar.copy(
                out=grouped[i // GROUP][:, i % GROUP].bitcast(F32),
                in_=xt[i][:].rearrange("p (g u) r -> p g r u", u=2),
            )

        def quantise_ff(n, first, last):
            if first == 0:
                ff_codes = quant.tile([P, GROUP * PASSES * P], U32, align_bytes=64)
                ff_scales = quant.tile([P, GROUP * PASSES * P], U8, align_bytes=64)
                codes[n] = (ff_codes, ff_scales)
            c = slice(first * PASSES * P, last * PASSES * P)
            nc.vector.quantize_mx(
                out=codes[n][0][:, c].bitcast(FP8X4),
                scales=codes[n][1][:, c],
                in_=grouped[n][:, first:last].rearrange("p j g r t -> p (j g r t)"),
            )

        def add_bias(i):
            rb[i] = rb_pool.tile([P, H], F32, name="rb")
            if i in VC:
                nc.vector.tensor_tensor(out=rb[i][:], in0=res_sb[i][:], in1=bias_bc[:], op=ALU.add)
                return
            if by_tensor(i):
                for h in range(HALVES):
                    ps = psum_acc.tile([P, BANK], F32, name="acc")
                    nc.tensor.matmul(out=ps[:], lhsT=ident_bf[:], rhs=res_sb[i][:, half(h)], start=True, stop=False)
                    if not BT or i in ONES:
                        nc.tensor.matmul(out=ps[:], lhsT=ones[:], rhs=rows["bias"][:, half(h)], start=False, stop=True)
                    for c in range(BANK // P if BT and i not in ONES else 0):
                        k = h * (BANK // P) + c
                        nc.tensor.matmul(
                            out=ps[:, c * P : (c + 1) * P],
                            lhsT=bias_turned[:, k, :],
                            rhs=ident[:],
                            is_transpose=True,
                            start=False,
                            stop=(c == BANK // P - 1),
                        )
                    nc.scalar.copy(out=rb[i][:, half(h)], in_=ps[:])
                return
            w = H // GSPLIT
            for s in range(GSPLIT):
                c = slice(s * w, s * w + w)
                nc.gpsimd.tensor_tensor(out=rb[i][:, c], in0=res_sb[i][:, c], in1=bias_bc[:, c], op=ALU.add)

        def project(i, halves=range(HALVES)):
            ff_codes, ff_scales = codes[i // GROUP]
            for h in halves:
                acc[i, h] = psum_acc.tile([P, BANK], F32, name="acc")
                for g in range(PASSES):
                    tok = slice(((i % GROUP) * PASSES + g) * P, ((i % GROUP) * PASSES + g + 1) * P)
                    nc.tensor.matmul_mx(
                        out=acc[i, h][:],
                        lhsT=ff_codes[:, tok].bitcast(FP8X4),
                        lhsT_scale=ff_scales[:, tok],
                        rhs=w_codes[g, h][:].bitcast(FP8X4),
                        rhs_scale=w_scales[g, h][:],
                        start=(g == 0),
                        stop=(g == PASSES - 1),
                    )

        def add_residual(i, h):
            if h == 0:
                u[i] = work.tile([P, H], F32, name="u")
                total[i] = stats.tile([P, HALVES], F32, name="total")
            if sum_on_vector(i):
                nc.vector.scalar_tensor_tensor(out=u[i][:, half(h)], in0=acc[i, h][:], scalar=1.0, in1=rb[i][:, half(h)], op0=ALU.mult, op1=ALU.add, accum_out=total[i][:, h:h+1])
            else:
                nc.vector.tensor_tensor(out=u[i][:, half(h)], in0=acc[i, h][:], in1=rb[i][:, half(h)], op=ALU.add)

        def mean(i):
            negmean[i] = stats.tile([P, 1], F32, name="negmean")
            if sum_on_vector(i):
                unused = stats.tile([P, HALVES], F32, name="unused2")
                nc.scalar.activation(out=unused[:], in_=total[i][:], func=ACT.Identity, scale=-1.0 / H, accum_out=negmean[i][:])
            else:
                unused = stats.tile([P, H], BF16, name="unused")
                nc.scalar.activation(out=unused[:], in_=u[i][:], func=ACT.Identity, scale=-1.0 / H, accum_out=negmean[i][:])

        def squared_deviations(i):
            ssq[i] = stats.tile([P, 1], F32, name="ssq")
            unused = stats.tile([P, H], BF16, name="unused")
            nc.scalar.activation(out=unused[:], in_=u[i][:], func=ACT.Square, bias=negmean[i][:], scale=1.0, accum_out=ssq[i][:])

        def inverse_deviation(i):
            rstd[i] = stats.tile([P, 1], F32, name="rstd")
            nc.scalar.activation(out=rstd[i][:], in_=ssq[i][:], func=ACT.Abs_reciprocal_sqrt, bias=eps_t[:], scale=1.0 / H)

        def centre_and_gain(i):
            y[i] = y_pool.tile([P, H], F32, name="y")
            nc.vector.scalar_tensor_tensor(out=y[i][:], in0=u[i][:], scalar=negmean[i][:], in1=vgain[0][:], op0=ALU.add, op1=ALU.mult)

        nmr = {}

        def centre(i):
            nmr[i] = stats.tile([P, 1], F32, name="nmr")
            nc.scalar.activation(out=nmr[i][:], in_=negmean[i][:], func=ACT.Copy, scale=rstd[i][:])

        def normalise(i):
            y[i] = y_pool.tile([P, H], F32, name="y")
            nc.scalar.activation(out=y[i][:], in_=u[i][:], func=ACT.Identity, scale=rstd[i][:], bias=nmr[i][:])

        def gain_only(i):
            w = H // GSPLIT
            for s in range(GSPLIT):
                c = slice(s * w, s * w + w)
                nc.gpsimd.tensor_tensor(out=y[i][:, c], in0=y[i][:, c], in1=gain_bc[:, c], op=ALU.mult)

        def scale_and_shift(i):
            nc.vector.scalar_tensor_tensor(out=y[i][:], in0=y[i][:], scalar=rstd[i][:], in1=vgain[1][:], op0=ALU.mult, op1=ALU.add)

        def scale_only(i):
            nc.scalar.activation(out=y[i][:], in_=y[i][:], func=ACT.Copy, scale=rstd[i][:])

        def shift_only(i):
            w = H // GSPLIT
            for s in range(GSPLIT):
                c = slice(s * w, s * w + w)
                nc.gpsimd.tensor_tensor(out=y[i][:, c], in0=y[i][:, c], in1=shift_bc[:, c], op=ALU.add)

        def store(i):
            nc.sync.dma_start(out=out_v[i], in_=y[i][:])

        rows = {}
        ident = const.tile([P, P], F32)
        make_identity(nc, ident[:])
        ident_bf = const.tile([P, P], BF16)
        nc.scalar.copy(out=ident_bf[:], in_=ident[:])
        ones = const.tile([P, P], BF16)
        nc.vector.memset(ones[:], 1.0)
        for name in ("bias", "gain", "shift"):
            rows[name] = const.tile([P, H], BF16, name="row_" + name)
            nc.vector.memset(rows[name][:].bitcast(I32), 0)
        eps_t = const.tile([P, 1], F32)
        nc.vector.memset(eps_t[:], EPS)
        warm = const.tile([P, 1], F32)
        nc.scalar.activation(out=warm[:], in_=eps_t[:], func=ACT.Abs_reciprocal_sqrt)

        def load_row(name, vec):
            nc.sync.dma_start(out=rows[name][0:1, :], in_=vec.rearrange("(o n) -> o n", o=1))

        def spread_row(name, h, out_ps):
            nc.tensor.matmul(out=out_ps, lhsT=ones[:], rhs=rows[name][:, half(h)], start=True, stop=True)

        w_raw, w_grp, w_codes, w_scales = {}, {}, {}, {}
        for h in range(HALVES):
            for g in range(PASSES):
                w_raw[g, h] = weights.tile([P, PACK, BANK], BF16, name="w_raw%d%d" % (g, h))
                w_grp[g, h] = weights.tile([P, BANK, PACK], BF16, align_bytes=64, name="w_grp%d%d" % (g, h))
                w_codes[g, h] = weights.tile([P, BANK], U32, align_bytes=64, name="w_codes%d%d" % (g, h))
                w_scales[g, h] = weights.tile([P, BANK], U8, align_bytes=64, name="w_scales%d%d" % (g, h))

        def load_w(g, h, part=None):
            if part is None:
                nc.sync.dma_start(out=w_raw[g, h][:], in_=w_v[g][:, :, half(h)])
            else:
                lo = h * BANK + part * (BANK // 2)
                nc.sync.dma_start(out=w_parts[part][:], in_=w_v[g][:, :, lo : lo + BANK // 2])

        if FIRST2:
            w_parts = {}
            for part in range(2):
                w_parts[part] = weights.tile([P, PACK, BANK // 2], BF16, name="w_part%d" % part)
            load_w(0, 0, 0)
            if BF:
                load_row("bias", b_f)
            load_w(0, 0, 1)
        else:
            load_w(0, 0)
            if BF:
                load_row("bias", b_f)
            if RE:
                load_row("gain", ln2_g)
                load_row("shift", ln2_b)
        load_ff(0)
        load_w(1, 0)
        load_ff(1)
        load_res(0)
        if not BF:
            load_row("bias", b_f)
        load_w(0, 1)
        load_w(1, 1)
        load_ff(2)
        load_ff(3)
        if not RE:
            load_row("gain", ln2_g)
            load_row("shift", ln2_b)
        for i in range(1, RES_AHEAD):
            load_res(i)
            if GROUP - 1 + i < FF_AHEAD:
                load_ff(GROUP - 1 + i)
        for i in range(GROUP - 1 + RES_AHEAD, FF_AHEAD):
            load_ff(i)
        bias_bc = const.tile([P, H], BF16)
        bias_turned = const.tile([P, H // P, P], F32)
        def spread_bias():
            for h in range(HALVES):
                bias_ps = psum_acc.tile([P, BANK], F32, name="acc")
                spread_row("bias", h, bias_ps[:])
                nc.scalar.copy(out=bias_bc[:, half(h)], in_=bias_ps[:])
        def turn_bias():
            turned = psum_t.tile([P, H // P, P], BF16, name="xt")
            for c in range(H // P):
                nc.tensor.transpose(turned[:, c, :], bias_bc[:, c * P : (c + 1) * P], ident_bf[:])
            nc.scalar.copy(out=bias_turned[:], in_=turned[:])

        def regroup_w(g, h):
            if FIRST2 and (g, h) == (0, 0):
                for part in range(2):
                    nc.vector.tensor_copy(
                        out=w_grp[g, h][:, part * (BANK // 2) : (part + 1) * (BANK // 2), :].rearrange("p (c i) t -> p c t i", i=4),
                        in_=w_parts[part][:].rearrange("p t (c i) -> p c t i", i=4),
                    )
                return
            dst = w_grp[g, h][:].rearrange("p (c i) t -> p c t i", i=4)
            src = w_raw[g, h][:].rearrange("p t (c i) -> p c t i", i=4)
            if (g, h) in SREG:
                nc.scalar.copy(out=dst, in_=src)
            else:
                nc.vector.tensor_copy(out=dst, in_=src)

        def quantise_w(g, h):
            nc.vector.quantize_mx(
                out=w_codes[g, h][:].bitcast(FP8X4),
                scales=w_scales[g, h][:],
                in_=w_grp[g, h][:].rearrange("p n t -> p (n t)"),
            )

        shift_bc = const.tile([P, H], BF16)
        if CP:
            gain_ps = psum_const.tile([P, H], BF16)
            shift_ps = psum_const.tile([P, H], BF16)
            vgain = (gain_ps, shift_ps)
        else:
            vgain = (gain_bc, shift_bc)

        def spread_rest():
            if CP:
                for h in range(HALVES):
                    spread_row("gain", h, gain_ps[:, half(h)])
                    spread_row("shift", h, shift_ps[:, half(h)])
                nc.scalar.copy(out=shift_bc[:], in_=shift_ps[:])
                nc.scalar.copy(out=gain_bc[:], in_=gain_ps[:])
            else:
                for name, dst in (("gain", gain_bc), ("shift", shift_bc)):
                    tp2 = psum_t.tile([P, H], BF16, name="xt")
                    for h in range(HALVES):
                        spread_row(name, h, tp2[:, half(h)])
                    nc.scalar.copy(out=dst[:], in_=tp2[:])
        done_first = set()
        done_d = set()
        for op in HEADSEQ.split():
            a = op[1:]
            if op[0] == "t":
                transpose(int(a))
                regroup(int(a))
                head_turned = int(a) + 1
            elif op[0] == "r":
                regroup_w(int(a[0]), int(a[1]))
            elif op[0] == "q":
                quantise_w(int(a[0]), int(a[1]))
            elif op[0] == "f":
                quantise_ff(0, int(a[0]), int(a[1]))
            elif op[0] == "b":
                add_bias(int(a))
            elif op[0] == "d":
                add_residual(int(a[0]), int(a[1]))
                done_d.add((int(a[0]), int(a[1])))
                if a[1] == "1":
                    mean(int(a[0]))
            elif op[0] == "p":
                project(int(a[0]), (int(a[1]),))
                done_first.add((int(a[0]), int(a[1])))
            elif op == "S":
                spread_bias()
            elif op == "R":
                spread_rest()
            elif op == "T":
                turn_bias()
        def tile_exists(i):
            return 0 <= i < N_TILES

        def prepared(i):
            return min(N_TILES, head_turned + 2 * i, i + PREP)

        for i in range(N_TILES + SHIFT_LAG):
            if tile_exists(i + FF_AHEAD):
                load_ff(i + FF_AHEAD)
            if tile_exists(i + RES_AHEAD):
                load_res(i + RES_AHEAD)
            if tile_exists(i + RB_AHEAD) and not by_tensor(i + RB_AHEAD) and i + RB_AHEAD not in rb and i + RB_AHEAD not in VC:
                add_bias(i + RB_AHEAD)
            if tile_exists(i):
                left = tuple(h for h in range(HALVES) if (i, h) not in done_first)
                if left:
                    project(i, left)
            for t in range(prepared(i), prepared(i + 1)):
                transpose(t)
                regroup(t)
            if i == REST_AT:
                spread_rest()
            if i == TB_AT:
                turn_bias()
            if tile_exists(i + RB_AHEAD) and by_tensor(i + RB_AHEAD) and i + RB_AHEAD not in rb and i + RB_AHEAD not in VC:
                add_bias(i + RB_AHEAD)
            if full(i - G2_LAG):
                normalise(i - G2_LAG)
            elif handed_over(i - G2_LAG):
                scale_only(i - G2_LAG)
            for what in ORDER.split(' '):
                if what == VCW and i + 1 in VC and i + 1 not in rb:
                    add_bias(i + 1)
                if what == 'd0' and tile_exists(i) and (i, 0) not in done_d:
                    add_residual(i, 0)
                if what == 'g1' and tile_exists(i - G1_LAG) and not full(i - G1_LAG):
                    centre_and_gain(i - G1_LAG)
                if what == 'd1' and tile_exists(i) and (i, 1) not in done_d:
                    add_residual(i, 1)
                    mean(i)
                if what == 'q':
                    if i == Q23:
                        quantise_ff(0, 2, 4)
                    elif i % GROUP == GROUP - QLEAD and tile_exists(i + QLEAD):
                        quantise_ff((i + QLEAD) // GROUP, 0, GROUP)
                if what == 'g2':
                    if tile_exists(i - 1):
                        inverse_deviation(i - 1)
                    if tile_exists(i):
                        squared_deviations(i)
                    if full(i - 1):
                        centre(i - 1)
                    t = i - G2_LAG
                    if t in LASTH:
                        for h in range(HALVES):
                            nc.vector.scalar_tensor_tensor(out=y[t][:, half(h)], in0=y[t][:, half(h)], scalar=rstd[t][:], in1=vgain[1][:, half(h)], op0=ALU.mult, op1=ALU.add)
                            nc.sync.dma_start(out=out_v[t][:, half(h)], in_=y[t][:, half(h)])
                    elif tile_exists(t) and not handed_over(t) and not full(t):
                        scale_and_shift(t)
                        store(t)
            if full(i - GAIN_LAG):
                gain_only(i - GAIN_LAG)
            if handed_over(i - SHIFT_LAG) or full(i - SHIFT_LAG):
                shift_only(i - SHIFT_LAG)
                if i - SHIFT_LAG != STORE_LAST:
                    store(i - SHIFT_LAG)
        if STORE_LAST >= 0:
            store(STORE_LAST)
